import numpy as np
import ml_dtypes


def mxq(x, axis, fmt="e4m3"):
    dtype, down = {"e4m3": (ml_dtypes.float8_e4m3fn, 7), "e5m2": (ml_dtypes.float8_e5m2, 14)}[fmt]
    v = np.moveaxis(np.asarray(x, np.float32).astype(ml_dtypes.bfloat16).astype(np.float64), axis, -1)
    blocks = v.reshape(v.shape[:-1] + (-1, 32))
    amax = np.abs(blocks).max(-1, keepdims=True)
    byte = np.maximum(np.where(amax > 0, np.frexp(amax)[1] - 1 + 127, 0) - down, 1)
    scale = np.exp2(byte - 127.0)
    codes = (blocks / scale).astype(np.float32).astype(dtype).astype(np.float64)
    return np.moveaxis((codes * scale).reshape(v.shape), -1, axis)


WIDE = False


def mx_kscale(k):
    if not WIDE:
        return np.ones(k)
    levels = np.array([10, -10, 5, -5, 0])
    a = np.random.permutation(np.resize(levels, k // 512 * 4)).reshape(k // 512, 4)
    idx = np.arange(k)
    return np.exp2(a[idx // 512, idx % 128 // 32])


BF16 = ml_dtypes.bfloat16


def bf(x):
    return np.asarray(x, np.float32).astype(BF16)


def f64(x):
    return np.asarray(x).astype(np.float64)


E2M1 = np.array([0.0, 0.5, 1.0, 1.5, 2.0, 3.0, 4.0, 6.0, -0.0, -0.5, -1.0, -1.5, -2.0, -3.0, -4.0, -6.0])


def pack_weight(w, fmt):
    k, n = w.shape
    w = f64(bf(w)).reshape(k // 32, 32, n)
    amax = np.abs(w).max(1)
    if fmt == "e4m3":
        byte = np.frexp(amax)[1] - 1 + 127 - 7
    else:
        mant, ex = np.frexp(amax / 6.0)
        byte = np.where(mant > 0.5, ex, ex - 1) + 127
    byte = np.clip(np.where(amax > 0, byte, 1), 1, 254)
    scaled = (w * np.exp2(127.0 - byte)[:, None, :]).reshape(k, n).astype(np.float32)
    by_word = np.ascontiguousarray(scaled.reshape(k // 512, 128, 4, n).transpose(0, 1, 3, 2))
    if fmt == "e4m3":
        words = by_word.astype(ml_dtypes.float8_e4m3fn).view(np.uint8)
    else:
        c = by_word.astype(ml_dtypes.float4_e2m1fn).view(np.uint8) & 0xF
        words = c[..., 0::2] | (c[..., 1::2] << 4)
    return np.ascontiguousarray(words), np.ascontiguousarray(byte.astype(np.uint8).reshape(k // 512, 16, n))


def unpack_weight(words, scales, fmt):
    g, p, n, _ = words.shape
    if fmt == "e4m3":
        vals = np.ascontiguousarray(words).view(ml_dtypes.float8_e4m3fn).astype(np.float64)
    else:
        nib = np.empty((g, p, n, 4), np.uint8)
        nib[..., 0::2] = words & 0xF
        nib[..., 1::2] = words >> 4
        vals = E2M1[nib]
    vals = vals * np.repeat(np.exp2(scales.astype(np.float64) - 127.0), 8, axis=1)[..., None]
    return vals.transpose(0, 1, 3, 2).reshape(g * 512, n)

def pack4(w):
    words, scales = pack_weight(w, "e2m1")
    return words.reshape(words.shape[0], 128, -1), scales


def unpack4(words, scales):
    return unpack_weight(words.reshape(words.shape[0], 128, -1, 2), scales, "e2m1")


B, T, D, F = 2, 512, 512, 512
BINS = np.array([-1.5, -1.0, -0.5, 0.0, 0.5, 1.0, 1.5])
NB = BINS.shape[0] + 1
INDEX = 0


def setup_inputs():
    s = mx_kscale(D)
    s = s / s[INDEX]
    x = bf(np.random.standard_normal((B, T, D)) * s)
    stack = np.random.standard_normal((NB, D, F)) * 0.5 / np.sqrt(D) / s[None, :, None]
    cat = stack.reshape(-1, F)
    words, scales = pack4(cat)
    return {"x": x, "W_words": words, "W_scales": scales}


def reference(x, W_words, W_scales):
    x = f64(x)
    y = x[..., INDEX]
    mem = np.sum(np.where(y[..., None] > BINS, 1.0, 0.0), axis=-1)
    xf = x.reshape(B * T, D)
    memf = mem.reshape(B * T)
    xq = mxq(xf, 1, "e4m3")
    Wq = unpack4(W_words, W_scales).reshape(NB, D, F)
    out = np.zeros((B * T, F))
    for k in range(NB):
        sel = np.where(memf == k, 1.0, 0.0)[:, None]
        out = out + sel * (xq @ Wq[k])
    return out.reshape(B, T, F)

@@ -1,0 +1,197 @@
+import concourse.mybir as mybir
+from concourse.masks import make_identity
+
+F32 = mybir.dt.float32
+BF16 = mybir.dt.bfloat16
+I32 = mybir.dt.int32
+U32 = mybir.dt.uint32
+U8 = mybir.dt.uint8
+FP8X4 = mybir.dt.float8_e4m3fn_x4
+FP4X4 = mybir.dt.float4_e2m1fn_x4
+ALU = mybir.AluOpType
+ACT = mybir.ActivationFunctionType
+
+P = 128
+TOKENS = 1024
+D = 512
+F = 512
+EDGES = (-1.5, -1.0, -0.5, 0.0, 0.5, 1.0, 1.5)
+EXPERTS = len(EDGES) + 1
+HALVES = 2
+BANKS = EXPERTS // HALVES
+TILES = TOKENS // P
+BUNCH = 2
+BUNCHES = TILES // BUNCH
+PSUM_BANKS = 8
+PAIRS = 2
+
+FLOPS = 2 * TOKENS * D * F * EXPERTS
+
+
+def tile_dispatchbyvariable_pa_e_kernel(tc, x, W_words, W_scales, out):
+    nc = tc.nc
+    x_rows = x.flatten_outer_dims().rearrange("(p j) d -> p j d", j=TILES)
+    out_rows = out.flatten_outer_dims().rearrange("(p j) f -> p j f", j=TILES)
+
+    with (
+        tc.tile_pool(name="keep", bufs=1) as keep,
+        tc.tile_pool(name="ring", bufs=2 * BUNCH) as ring,
+        tc.psum_pool(name="flip_banks", bufs=BUNCH) as flip_banks,
+        tc.psum_pool(name="sum_banks", bufs=PSUM_BANKS - BUNCH) as sum_banks,
+        tc.manual_schedule(),
+    ):
+        x_sb = keep.tile([P, TILES, D], BF16)
+        w_words = keep.tile([P, EXPERTS, 2 * F], U8, align_bytes=64)
+        w_planes = keep.tile([P, EXPERTS, F], U8, align_bytes=64)
+        identity = keep.tile([P, P], F32)
+        edges = keep.tile([P, len(EDGES)], F32)
+        above = keep.tile([P, TILES, EXPERTS + 1], F32)
+        one_hot = keep.tile([P, TILES, EXPERTS], F32)
+        bank_pick = keep.tile([P, TILES, BANKS], F32)
+        half_pick = keep.tile([P, TILES, HALVES], F32)
+
+        nc.vector.memset(w_planes[:].rearrange("p g n -> p (g n)").bitcast(I32), 0)
+        for k, edge in enumerate(EDGES):
+            nc.vector.memset(edges[:, k : k + 1], edge)
+        nc.vector.memset(above[:, :, 0:1], 1.0)
+        nc.vector.memset(above[:, :, EXPERTS : EXPERTS + 1], 0.0)
+        make_identity(nc, identity[:])
+
+        def load_x(bunch):
+            tiles = slice(bunch * BUNCH, (bunch + 1) * BUNCH)
+            nc.sync.dma_start(out=x_sb[:, tiles, :], in_=x_rows[:, tiles, :])
+
+        load_x(0)
+        load_x(1)
+        for low_q in range(2):
+            for r in range(4):
+                nc.sync.dma_start(
+                    out=w_planes[32 * low_q + r : P : 64, :, :].bitcast(I32),
+                    in_=W_scales[:, 4 * low_q + r : 16 : 8, :]
+                    .bitcast(I32)
+                    .rearrange("g q n -> q g n"),
+                )
+        for bank in range(BANKS):
+            nc.sync.dma_start(
+                out=w_words[:, bank:EXPERTS:BANKS, :].bitcast(I32),
+                in_=W_words[bank:EXPERTS:BANKS].bitcast(I32).rearrange("g p b -> p g b"),
+            )
+        for bunch in range(2, BUNCHES):
+            load_x(bunch)
+
+        sorted_of = {}
+        gates_of = {}
+        codes_of = {}
+        scales_of = {}
+
+        def select_and_sort(bunch):
+            tiles = slice(bunch * BUNCH, (bunch + 1) * BUNCH)
+            shape = [P, BUNCH, len(EDGES)]
+            nc.vector.tensor_tensor(
+                out=above[:, tiles, 1:EXPERTS],
+                in0=x_sb[:, tiles, 0:1].to_broadcast(shape),
+                in1=edges[:].unsqueeze(1).to_broadcast(shape),
+                op=ALU.is_gt,
+            )
+            nc.vector.tensor_sub(
+                out=half_pick[:, tiles, :],
+                in0=above[:, tiles, 0:EXPERTS:BANKS],
+                in1=above[:, tiles, BANKS : EXPERTS + 1 : BANKS],
+            )
+            nc.vector.tensor_sub(
+                out=one_hot[:, tiles, :],
+                in0=above[:, tiles, 0:EXPERTS],
+                in1=above[:, tiles, 1 : EXPERTS + 1],
+            )
+            nc.vector.tensor_add(
+                out=bank_pick[:, tiles, :],
+                in0=one_hot[:, tiles, 0:BANKS],
+                in1=one_hot[:, tiles, BANKS:EXPERTS],
+            )
+            for j in range(bunch * BUNCH, (bunch + 1) * BUNCH):
+                sorted_words = ring.tile([P, PAIRS, P], F32)
+                nc.scalar.copy(
+                    out=sorted_words[:],
+                    in_=x_sb[:, j, :].bitcast(F32).rearrange("p (w u) -> p u w", u=PAIRS),
+                )
+                sorted_of[j] = sorted_words
+                gates = ring.tile([P, HALVES, P], F32)
+                for half in range(HALVES):
+                    nc.gpsimd.tensor_scalar(
+                        out=gates[:, half, :],
+                        in0=identity[:],
+                        scalar1=half_pick[:, j, half : half + 1],
+                        scalar2=0.0,
+                        op0=ALU.mult,
+                        op1=ALU.add,
+                    )
+                gates_of[j] = gates
+
+        def flip_and_quantise(bunch):
+            flipped_of = {}
+            for j in range(bunch * BUNCH, (bunch + 1) * BUNCH):
+                flipped = flip_banks.tile([P, HALVES, PAIRS, P], F32)
+                for half in range(HALVES):
+                    for u in range(PAIRS):
+                        nc.tensor.transpose(
+                            out=flipped[:, half, u, :],
+                            in_=sorted_of[j][:, u, :],
+                            identity=gates_of[j][:, half, :],
+                        )
+                flipped_of[j] = flipped
+            for j in range(bunch * BUNCH, (bunch + 1) * BUNCH):
+                grouped = ring.tile([P, HALVES * P * 2 * PAIRS], BF16, align_bytes=64)
+                nc.scalar.copy(
+                    out=grouped[:]
+                    .bitcast(F32)
+                    .rearrange("p (h r u) -> p h r u", h=HALVES, u=PAIRS),
+                    in_=flipped_of[j][:].rearrange("p h u r -> p h r u"),
+                )
+                codes = ring.tile([P, HALVES * P], U32, align_bytes=64)
+                scales = ring.tile([P, HALVES * P], U8, align_bytes=64)
+                nc.vector.quantize_mx(
+                    out=codes[:].bitcast(FP8X4), scales=scales[:], in_=grouped[:]
+                )
+                codes_of[j] = codes
+                scales_of[j] = scales
+
+        def multiply(j):
+            result = ring.tile([P, F], F32)
+            for bank in range(BANKS):
+                sums = sum_banks.tile([P, F], F32)
+                for half in range(HALVES):
+                    tokens = slice(half * P, (half + 1) * P)
+                    expert = half * BANKS + bank
+                    nc.tensor.matmul_mx(
+                        out=sums[:],
+                        lhsT=codes_of[j][:, tokens].bitcast(FP8X4),
+                        lhsT_scale=scales_of[j][:, tokens],
+                        rhs=w_words[:, expert, :].bitcast(FP4X4),
+                        rhs_scale=w_planes[:, expert, :],
+                        start=(half == 0),
+                        stop=(half == HALVES - 1),
+                    )
+                pick = bank_pick[:, j, bank : bank + 1]
+                if bank == 0:
+                    nc.scalar.activation(out=result[:], in_=sums[:], func=ACT.Copy, scale=pick)
+                else:
+                    nc.vector.scalar_tensor_tensor(
+                        out=result[:],
+                        in0=sums[:],
+                        scalar=pick,
+                        in1=result[:],
+                        op0=ALU.mult,
+                        op1=ALU.add,
+                    )
+            nc.sync.dma_start(out=out_rows[:, j, :], in_=result[:])
+
+        select_and_sort(0)
+        flip_and_quantise(0)
+        select_and_sort(1)
+        for bunch in range(BUNCHES):
+            multiply(bunch * BUNCH)
+            if bunch + 1 < BUNCHES:
+                flip_and_quantise(bunch + 1)
+            multiply(bunch * BUNCH + 1)
+            if bunch + 2 < BUNCHES:
+                select_and_sort(bunch + 2)

@@ -36,6 +36,7 @@ def tile_dispatchbyvariable_pa_e_kernel(tc, x, W_words, W_scales, out):
     with (
         tc.tile_pool(name="keep", bufs=1) as keep,
         tc.tile_pool(name="ring", bufs=2 * BUNCH) as ring,
+        tc.tile_pool(name="partials", bufs=4 * BUNCH) as partials,
         tc.psum_pool(name="flip_banks", bufs=BUNCH) as flip_banks,
         tc.psum_pool(name="sum_banks", bufs=PSUM_BANKS - BUNCH) as sum_banks,
         tc.manual_schedule(),
@@ -156,7 +157,7 @@ def tile_dispatchbyvariable_pa_e_kernel(tc, x, W_words, W_scales, out):
                 scales_of[j] = scales
 
         def multiply(j):
-            result = ring.tile([P, F], F32)
+            partial_of = {}
             for bank in range(BANKS):
                 sums = sum_banks.tile([P, F], F32)
                 for half in range(HALVES):
@@ -172,26 +173,31 @@ def tile_dispatchbyvariable_pa_e_kernel(tc, x, W_words, W_scales, out):
                         stop=(half == HALVES - 1),
                     )
                 pick = bank_pick[:, j, bank : bank + 1]
-                if bank == 0:
-                    nc.scalar.activation(out=result[:], in_=sums[:], func=ACT.Copy, scale=pick)
+                if bank % 2 == 0:
+                    partial = partials.tile([P, F], F32)
+                    nc.scalar.activation(out=partial[:], in_=sums[:], func=ACT.Copy, scale=pick)
+                    partial_of[bank // 2] = partial
                 else:
                     nc.vector.scalar_tensor_tensor(
-                        out=result[:],
+                        out=partial_of[bank // 2][:],
                         in0=sums[:],
                         scalar=pick,
-                        in1=result[:],
+                        in1=partial_of[bank // 2][:],
                         op0=ALU.mult,
                         op1=ALU.add,
                     )
-            nc.sync.dma_start(out=out_rows[:, j, :], in_=result[:])
+            nc.gpsimd.tensor_tensor(
+                out=partial_of[0][:], in0=partial_of[0][:], in1=partial_of[1][:], op=ALU.add
+            )
+            nc.sync.dma_start(out=out_rows[:, j, :], in_=partial_of[0][:])
 
         select_and_sort(0)
         flip_and_quantise(0)
         select_and_sort(1)
         for bunch in range(BUNCHES):
             multiply(bunch * BUNCH)
+            if bunch + 2 < BUNCHES:
+                select_and_sort(bunch + 2)
             if bunch + 1 < BUNCHES:
                 flip_and_quantise(bunch + 1)
             multiply(bunch * BUNCH + 1)
-            if bunch + 2 < BUNCHES:
-                select_and_sort(bunch + 2)

@@ -35,10 +35,9 @@ def tile_dispatchbyvariable_pa_e_kernel(tc, x, W_words, W_scales, out):
 
     with (
         tc.tile_pool(name="keep", bufs=1) as keep,
-        tc.tile_pool(name="ring", bufs=2 * BUNCH) as ring,
+        tc.tile_pool(name="ring", bufs=3 * BUNCH) as ring,
         tc.tile_pool(name="partials", bufs=4 * BUNCH) as partials,
-        tc.psum_pool(name="flip_banks", bufs=BUNCH) as flip_banks,
-        tc.psum_pool(name="sum_banks", bufs=PSUM_BANKS - BUNCH) as sum_banks,
+        tc.psum_pool(name="banks", bufs=PSUM_BANKS) as banks,
         tc.manual_schedule(),
     ):
         x_sb = keep.tile([P, TILES, D], BF16)
@@ -99,6 +98,21 @@ def tile_dispatchbyvariable_pa_e_kernel(tc, x, W_words, W_scales, out):
                 in0=above[:, tiles, 0:EXPERTS:BANKS],
                 in1=above[:, tiles, BANKS : EXPERTS + 1 : BANKS],
             )
+            for j in range(bunch * BUNCH, (bunch + 1) * BUNCH):
+                sorted_words = ring.tile([P, PAIRS, P], F32)
+                nc.scalar.copy(
+                    out=sorted_words[:],
+                    in_=x_sb[:, j, :].bitcast(F32).rearrange("p (w u) -> p u w", u=PAIRS),
+                )
+                sorted_of[j] = sorted_words
+                gates = ring.tile([P, HALVES, P], F32)
+                for half in range(HALVES):
+                    nc.vector.tensor_scalar_mul(
+                        out=gates[:, half, :],
+                        in0=identity[:],
+                        scalar1=half_pick[:, j, half : half + 1],
+                    )
+                gates_of[j] = gates
             nc.vector.tensor_sub(
                 out=one_hot[:, tiles, :],
                 in0=above[:, tiles, 0:EXPERTS],
@@ -109,29 +123,11 @@ def tile_dispatchbyvariable_pa_e_kernel(tc, x, W_words, W_scales, out):
                 in0=one_hot[:, tiles, 0:BANKS],
                 in1=one_hot[:, tiles, BANKS:EXPERTS],
             )
-            for j in range(bunch * BUNCH, (bunch + 1) * BUNCH):
-                sorted_words = ring.tile([P, PAIRS, P], F32)
-                nc.scalar.copy(
-                    out=sorted_words[:],
-                    in_=x_sb[:, j, :].bitcast(F32).rearrange("p (w u) -> p u w", u=PAIRS),
-                )
-                sorted_of[j] = sorted_words
-                gates = ring.tile([P, HALVES, P], F32)
-                for half in range(HALVES):
-                    nc.gpsimd.tensor_scalar(
-                        out=gates[:, half, :],
-                        in0=identity[:],
-                        scalar1=half_pick[:, j, half : half + 1],
-                        scalar2=0.0,
-                        op0=ALU.mult,
-                        op1=ALU.add,
-                    )
-                gates_of[j] = gates
 
         def flip_and_quantise(bunch):
             flipped_of = {}
             for j in range(bunch * BUNCH, (bunch + 1) * BUNCH):
-                flipped = flip_banks.tile([P, HALVES, PAIRS, P], F32)
+                flipped = banks.tile([P, HALVES, PAIRS, P], F32, tag="bank")
                 for half in range(HALVES):
                     for u in range(PAIRS):
                         nc.tensor.transpose(
@@ -159,7 +155,7 @@ def tile_dispatchbyvariable_pa_e_kernel(tc, x, W_words, W_scales, out):
         def multiply(j):
             partial_of = {}
             for bank in range(BANKS):
-                sums = sum_banks.tile([P, F], F32)
+                sums = banks.tile([P, F], F32, tag="bank")
                 for half in range(HALVES):
                     tokens = slice(half * P, (half + 1) * P)
                     expert = half * BANKS + bank
@@ -173,31 +169,33 @@ def tile_dispatchbyvariable_pa_e_kernel(tc, x, W_words, W_scales, out):
                         stop=(half == HALVES - 1),
                     )
                 pick = bank_pick[:, j, bank : bank + 1]
-                if bank % 2 == 0:
+                if bank < 2:
                     partial = partials.tile([P, F], F32)
                     nc.scalar.activation(out=partial[:], in_=sums[:], func=ACT.Copy, scale=pick)
-                    partial_of[bank // 2] = partial
+                    partial_of[bank] = partial
                 else:
                     nc.vector.scalar_tensor_tensor(
-                        out=partial_of[bank // 2][:],
+                        out=partial_of[bank - 2][:],
                         in0=sums[:],
                         scalar=pick,
-                        in1=partial_of[bank // 2][:],
+                        in1=partial_of[bank - 2][:],
                         op0=ALU.mult,
                         op1=ALU.add,
                     )
-            nc.gpsimd.tensor_tensor(
+            joiner = nc.vector if j == TILES - 1 else nc.gpsimd
+            joiner.tensor_tensor(
                 out=partial_of[0][:], in0=partial_of[0][:], in1=partial_of[1][:], op=ALU.add
             )
             nc.sync.dma_start(out=out_rows[:, j, :], in_=partial_of[0][:])
 
         select_and_sort(0)
-        flip_and_quantise(0)
         select_and_sort(1)
+        flip_and_quantise(0)
+        flip_and_quantise(1)
         for bunch in range(BUNCHES):
             multiply(bunch * BUNCH)
             if bunch + 2 < BUNCHES:
                 select_and_sort(bunch + 2)
-            if bunch + 1 < BUNCHES:
-                flip_and_quantise(bunch + 1)
             multiply(bunch * BUNCH + 1)
+            if bunch + 2 < BUNCHES:
+                flip_and_quantise(bunch + 2)

@@ -38,7 +38,6 @@ def tile_dispatchbyvariable_pa_e_kernel(tc, x, W_words, W_scales, out):
         tc.tile_pool(name="ring", bufs=3 * BUNCH) as ring,
         tc.tile_pool(name="partials", bufs=4 * BUNCH) as partials,
         tc.psum_pool(name="banks", bufs=PSUM_BANKS) as banks,
-        tc.manual_schedule(),
     ):
         x_sb = keep.tile([P, TILES, D], BF16)
         w_words = keep.tile([P, EXPERTS, 2 * F], U8, align_bytes=64)

@@ -17,6 +17,7 @@ D = 512
 F = 512
 EDGES = (-1.5, -1.0, -0.5, 0.0, 0.5, 1.0, 1.5)
 EXPERTS = len(EDGES) + 1
+MIDDLE_EDGE = EDGES[len(EDGES) // 2]
 HALVES = 2
 BANKS = EXPERTS // HALVES
 TILES = TOKENS // P
@@ -47,7 +48,6 @@ def tile_dispatchbyvariable_pa_e_kernel(tc, x, W_words, W_scales, out):
         above = keep.tile([P, TILES, EXPERTS + 1], F32)
         one_hot = keep.tile([P, TILES, EXPERTS], F32)
         bank_pick = keep.tile([P, TILES, BANKS], F32)
-        half_pick = keep.tile([P, TILES, HALVES], F32)
 
         nc.vector.memset(w_planes[:].rearrange("p g n -> p (g n)").bitcast(I32), 0)
         for k, edge in enumerate(EDGES):
@@ -92,11 +92,6 @@ def tile_dispatchbyvariable_pa_e_kernel(tc, x, W_words, W_scales, out):
                 in1=edges[:].unsqueeze(1).to_broadcast(shape),
                 op=ALU.is_gt,
             )
-            nc.vector.tensor_sub(
-                out=half_pick[:, tiles, :],
-                in0=above[:, tiles, 0:EXPERTS:BANKS],
-                in1=above[:, tiles, BANKS : EXPERTS + 1 : BANKS],
-            )
             for j in range(bunch * BUNCH, (bunch + 1) * BUNCH):
                 sorted_words = ring.tile([P, PAIRS, P], F32)
                 nc.scalar.copy(
@@ -105,12 +100,21 @@ def tile_dispatchbyvariable_pa_e_kernel(tc, x, W_words, W_scales, out):
                 )
                 sorted_of[j] = sorted_words
                 gates = ring.tile([P, HALVES, P], F32)
-                for half in range(HALVES):
-                    nc.vector.tensor_scalar_mul(
-                        out=gates[:, half, :],
-                        in0=identity[:],
-                        scalar1=half_pick[:, j, half : half + 1],
-                    )
+                nc.vector.tensor_scalar(
+                    out=gates[:, 1, :],
+                    in0=identity[:],
+                    scalar1=x_sb[:, j, 0:1],
+                    scalar2=MIDDLE_EDGE,
+                    op0=ALU.mult,
+                    op1=ALU.is_gt,
+                )
+                nc.vector.tensor_scalar(
+                    out=gates[:, 0, :],
+                    in0=identity[:],
+                    scalar1=above[:, j, BANKS : BANKS + 1],
+                    scalar2=None,
+                    op0=ALU.is_gt,
+                )
                 gates_of[j] = gates
             nc.vector.tensor_sub(
                 out=one_hot[:, tiles, :],
@@ -127,7 +131,7 @@ def tile_dispatchbyvariable_pa_e_kernel(tc, x, W_words, W_scales, out):
             flipped_of = {}
             for j in range(bunch * BUNCH, (bunch + 1) * BUNCH):
                 flipped = banks.tile([P, HALVES, PAIRS, P], F32, tag="bank")
-                for half in range(HALVES):
+                for half in reversed(range(HALVES)):
                     for u in range(PAIRS):
                         nc.tensor.transpose(
                             out=flipped[:, half, u, :],
@@ -181,20 +185,60 @@ def tile_dispatchbyvariable_pa_e_kernel(tc, x, W_words, W_scales, out):
                         op0=ALU.mult,
                         op1=ALU.add,
                     )
-            joiner = nc.vector if j == TILES - 1 else nc.gpsimd
-            joiner.tensor_tensor(
+            nc.gpsimd.tensor_tensor(
                 out=partial_of[0][:], in0=partial_of[0][:], in1=partial_of[1][:], op=ALU.add
             )
             nc.sync.dma_start(out=out_rows[:, j, :], in_=partial_of[0][:])
+
+        def multiply_last_bunch(tiles):
+            partial_of = {}
+            for bank in range(BANKS):
+                for j in tiles:
+                    sums = banks.tile([P, F], F32, tag="bank")
+                    for half in range(HALVES):
+                        tokens = slice(half * P, (half + 1) * P)
+                        expert = half * BANKS + bank
+                        nc.tensor.matmul_mx(
+                            out=sums[:],
+                            lhsT=codes_of[j][:, tokens].bitcast(FP8X4),
+                            lhsT_scale=scales_of[j][:, tokens],
+                            rhs=w_words[:, expert, :].bitcast(FP4X4),
+                            rhs_scale=w_planes[:, expert, :],
+                            start=(half == 0),
+                            stop=(half == HALVES - 1),
+                        )
+                    pick = bank_pick[:, j, bank : bank + 1]
+                    if bank == 0:
+                        partial = partials.tile([P, F], F32)
+                        nc.scalar.activation(
+                            out=partial[:], in_=sums[:], func=ACT.Copy, scale=pick
+                        )
+                        partial_of[j] = partial
+                    very_last = bank == BANKS - 1 and j == tiles[-1]
+                    pieces = (slice(0, F // 2), slice(F // 2, F)) if very_last else (slice(0, F),)
+                    for cols in pieces if bank > 0 else ():
+                        nc.vector.scalar_tensor_tensor(
+                            out=partial_of[j][:, cols],
+                            in0=sums[:, cols],
+                            scalar=pick,
+                            in1=partial_of[j][:, cols],
+                            op0=ALU.mult,
+                            op1=ALU.add,
+                        )
+                        if bank == BANKS - 1:
+                            nc.sync.dma_start(
+                                out=out_rows[:, j, cols], in_=partial_of[j][:, cols]
+                            )
 
         select_and_sort(0)
         select_and_sort(1)
         flip_and_quantise(0)
         flip_and_quantise(1)
-        for bunch in range(BUNCHES):
+        for bunch in range(BUNCHES - 1):
             multiply(bunch * BUNCH)
             if bunch + 2 < BUNCHES:
                 select_and_sort(bunch + 2)
             multiply(bunch * BUNCH + 1)
             if bunch + 2 < BUNCHES:
                 flip_and_quantise(bunch + 2)
+        multiply_last_bunch((TILES - 2, TILES - 1))

@@ -24,6 +24,7 @@ TILES = TOKENS // P
 BUNCH = 2
 BUNCHES = TILES // BUNCH
 PSUM_BANKS = 8
+WARM_UP = 4
 PAIRS = 2
 
 FLOPS = 2 * TOKENS * D * F * EXPERTS
@@ -49,12 +50,21 @@ def tile_dispatchbyvariable_pa_e_kernel(tc, x, W_words, W_scales, out):
         one_hot = keep.tile([P, TILES, EXPERTS], F32)
         bank_pick = keep.tile([P, TILES, BANKS], F32)
 
+        zeros = keep.tile([P, F], BF16)
+        nc.gpsimd.memset(zeros[:], 0.0)
         nc.vector.memset(w_planes[:].rearrange("p g n -> p (g n)").bitcast(I32), 0)
         for k, edge in enumerate(EDGES):
             nc.vector.memset(edges[:, k : k + 1], edge)
         nc.vector.memset(above[:, :, 0:1], 1.0)
         nc.vector.memset(above[:, :, EXPERTS : EXPERTS + 1], 0.0)
         make_identity(nc, identity[:])
+        unread = banks.tile([P, F], F32, tag="bank")
+
+        def keep_warm(count):
+            for i in range(count):
+                nc.tensor.matmul(
+                    out=unread[:], lhsT=zeros[:, 0:P], rhs=zeros[:], start=True, stop=True
+                )
 
         def load_x(bunch):
             tiles = slice(bunch * BUNCH, (bunch + 1) * BUNCH)
@@ -127,7 +137,7 @@ def tile_dispatchbyvariable_pa_e_kernel(tc, x, W_words, W_scales, out):
                 in1=one_hot[:, tiles, BANKS:EXPERTS],
             )
 
-        def flip_and_quantise(bunch):
+        def flip_and_quantise(bunch, fillers=0):
             flipped_of = {}
             for j in range(bunch * BUNCH, (bunch + 1) * BUNCH):
                 flipped = banks.tile([P, HALVES, PAIRS, P], F32, tag="bank")
@@ -139,6 +149,7 @@ def tile_dispatchbyvariable_pa_e_kernel(tc, x, W_words, W_scales, out):
                             identity=gates_of[j][:, half, :],
                         )
                 flipped_of[j] = flipped
+                keep_warm(fillers)
             for j in range(bunch * BUNCH, (bunch + 1) * BUNCH):
                 grouped = ring.tile([P, HALVES * P * 2 * PAIRS], BF16, align_bytes=64)
                 nc.scalar.copy(
@@ -230,10 +241,12 @@ def tile_dispatchbyvariable_pa_e_kernel(tc, x, W_words, W_scales, out):
                                 out=out_rows[:, j, cols], in_=partial_of[j][:, cols]
                             )
 
-        select_and_sort(0)
-        select_and_sort(1)
-        flip_and_quantise(0)
-        flip_and_quantise(1)
+        with tc.manual_schedule(engines={mybir.EngineType.PE}):
+            keep_warm(WARM_UP)
+            select_and_sort(0)
+            select_and_sort(1)
+            flip_and_quantise(0, fillers=1)
+            flip_and_quantise(1)
         for bunch in range(BUNCHES - 1):
             multiply(bunch * BUNCH)
             if bunch + 2 < BUNCHES:

@@ -72,14 +72,11 @@ def tile_dispatchbyvariable_pa_e_kernel(tc, x, W_words, W_scales, out):
 
         load_x(0)
         load_x(1)
-        for low_q in range(2):
-            for r in range(4):
-                nc.sync.dma_start(
-                    out=w_planes[32 * low_q + r : P : 64, :, :].bitcast(I32),
-                    in_=W_scales[:, 4 * low_q + r : 16 : 8, :]
-                    .bitcast(I32)
-                    .rearrange("g q n -> q g n"),
-                )
+        for r in range(4):
+            nc.sync.dma_start(
+                out=w_planes[r:P:32, :, :].bitcast(I32),
+                in_=W_scales[:, r:16:4, :].bitcast(I32).rearrange("g q n -> q g n"),
+            )
         for bank in range(BANKS):
             nc.sync.dma_start(
                 out=w_words[:, bank:EXPERTS:BANKS, :].bitcast(I32),

@@ -70,20 +70,29 @@ def tile_dispatchbyvariable_pa_e_kernel(tc, x, W_words, W_scales, out):
             tiles = slice(bunch * BUNCH, (bunch + 1) * BUNCH)
             nc.sync.dma_start(out=x_sb[:, tiles, :], in_=x_rows[:, tiles, :])
 
-        load_x(0)
-        load_x(1)
-        for r in range(4):
-            nc.sync.dma_start(
-                out=w_planes[r:P:32, :, :].bitcast(I32),
-                in_=W_scales[:, r:16:4, :].bitcast(I32).rearrange("g q n -> q g n"),
-            )
-        for bank in range(BANKS):
-            nc.sync.dma_start(
-                out=w_words[:, bank:EXPERTS:BANKS, :].bitcast(I32),
-                in_=W_words[bank:EXPERTS:BANKS].bitcast(I32).rearrange("g p b -> p g b"),
-            )
-        for bunch in range(2, BUNCHES):
-            load_x(bunch)
+        with tc.manual_schedule(engines={mybir.EngineType.SP}):
+            load_x(0)
+            load_x(1)
+            for r in range(2):
+                nc.sync.dma_start(
+                    out=w_planes[r:P:32, :, :].bitcast(I32),
+                    in_=W_scales[:, r:16:4, :].bitcast(I32).rearrange("g q n -> q g n"),
+                )
+            for r in range(2, 4):
+                for low_q in range(2):
+                    nc.sync.dma_start(
+                        out=w_planes[32 * low_q + r : P : 64, :, :].bitcast(I32),
+                        in_=W_scales[:, 4 * low_q + r : 16 : 8, :]
+                        .bitcast(I32)
+                        .rearrange("g q n -> q g n"),
+                    )
+            for bank in range(BANKS):
+                nc.sync.dma_start(
+                    out=w_words[:, bank:EXPERTS:BANKS, :].bitcast(I32),
+                    in_=W_words[bank:EXPERTS:BANKS].bitcast(I32).rearrange("g p b -> p g b"),
+                )
+            for bunch in range(2, BUNCHES):
+                load_x(bunch)
 
         sorted_of = {}
         gates_of = {}

@@ -96,10 +96,12 @@ def tile_dispatchbyvariable_pa_e_kernel(tc, x, W_words, W_scales, out):
 
         sorted_of = {}
         gates_of = {}
+        flipped_of = {}
+        grouped_of = {}
         codes_of = {}
         scales_of = {}
 
-        def select_and_sort(bunch):
+        def compare(bunch):
             tiles = slice(bunch * BUNCH, (bunch + 1) * BUNCH)
             shape = [P, BUNCH, len(EDGES)]
             nc.vector.tensor_tensor(
@@ -108,30 +110,36 @@ def tile_dispatchbyvariable_pa_e_kernel(tc, x, W_words, W_scales, out):
                 in1=edges[:].unsqueeze(1).to_broadcast(shape),
                 op=ALU.is_gt,
             )
-            for j in range(bunch * BUNCH, (bunch + 1) * BUNCH):
-                sorted_words = ring.tile([P, PAIRS, P], F32)
-                nc.scalar.copy(
-                    out=sorted_words[:],
-                    in_=x_sb[:, j, :].bitcast(F32).rearrange("p (w u) -> p u w", u=PAIRS),
-                )
-                sorted_of[j] = sorted_words
-                gates = ring.tile([P, HALVES, P], F32)
-                nc.vector.tensor_scalar(
-                    out=gates[:, 1, :],
-                    in0=identity[:],
-                    scalar1=x_sb[:, j, 0:1],
-                    scalar2=MIDDLE_EDGE,
-                    op0=ALU.mult,
-                    op1=ALU.is_gt,
-                )
-                nc.vector.tensor_scalar(
-                    out=gates[:, 0, :],
-                    in0=identity[:],
-                    scalar1=above[:, j, BANKS : BANKS + 1],
-                    scalar2=None,
-                    op0=ALU.is_gt,
-                )
-                gates_of[j] = gates
+
+        def sort_words(j, copy):
+            sorted_words = ring.tile([P, PAIRS, P], F32)
+            copy(
+                out=sorted_words[:],
+                in_=x_sb[:, j, :].bitcast(F32).rearrange("p (w u) -> p u w", u=PAIRS),
+            )
+            sorted_of[j] = sorted_words
+
+        def make_gates(j):
+            gates = ring.tile([P, HALVES, P], F32)
+            nc.vector.tensor_scalar(
+                out=gates[:, 1, :],
+                in0=identity[:],
+                scalar1=x_sb[:, j, 0:1],
+                scalar2=MIDDLE_EDGE,
+                op0=ALU.mult,
+                op1=ALU.is_gt,
+            )
+            nc.vector.tensor_scalar(
+                out=gates[:, 0, :],
+                in0=identity[:],
+                scalar1=above[:, j, BANKS : BANKS + 1],
+                scalar2=None,
+                op0=ALU.is_gt,
+            )
+            gates_of[j] = gates
+
+        def make_picks(bunch):
+            tiles = slice(bunch * BUNCH, (bunch + 1) * BUNCH)
             nc.vector.tensor_sub(
                 out=one_hot[:, tiles, :],
                 in0=above[:, tiles, 0:EXPERTS],
@@ -143,34 +151,49 @@ def tile_dispatchbyvariable_pa_e_kernel(tc, x, W_words, W_scales, out):
                 in1=one_hot[:, tiles, BANKS:EXPERTS],
             )
 
-        def flip_and_quantise(bunch, fillers=0):
-            flipped_of = {}
+        def select_and_sort(bunch):
+            compare(bunch)
             for j in range(bunch * BUNCH, (bunch + 1) * BUNCH):
-                flipped = banks.tile([P, HALVES, PAIRS, P], F32, tag="bank")
-                for half in reversed(range(HALVES)):
-                    for u in range(PAIRS):
-                        nc.tensor.transpose(
-                            out=flipped[:, half, u, :],
-                            in_=sorted_of[j][:, u, :],
-                            identity=gates_of[j][:, half, :],
-                        )
-                flipped_of[j] = flipped
-                keep_warm(fillers)
+                sort_words(j, nc.scalar.copy)
+                make_gates(j)
+            make_picks(bunch)
+
+        def flip(j):
+            flipped = banks.tile([P, HALVES, PAIRS, P], F32, tag="bank")
+            for half in reversed(range(HALVES)):
+                for u in range(PAIRS):
+                    nc.tensor.transpose(
+                        out=flipped[:, half, u, :],
+                        in_=sorted_of[j][:, u, :],
+                        identity=gates_of[j][:, half, :],
+                    )
+            flipped_of[j] = flipped
+
+        def group(j, copy):
+            grouped = ring.tile([P, HALVES * P * 2 * PAIRS], BF16, align_bytes=64)
+            copy(
+                out=grouped[:]
+                .bitcast(F32)
+                .rearrange("p (h r u) -> p h r u", h=HALVES, u=PAIRS),
+                in_=flipped_of[j][:].rearrange("p h u r -> p h r u"),
+            )
+            grouped_of[j] = grouped
+
+        def quantise(j):
+            codes = ring.tile([P, HALVES * P], U32, align_bytes=64)
+            scales = ring.tile([P, HALVES * P], U8, align_bytes=64)
+            nc.vector.quantize_mx(
+                out=codes[:].bitcast(FP8X4), scales=scales[:], in_=grouped_of[j][:]
+            )
+            codes_of[j] = codes
+            scales_of[j] = scales
+
+        def flip_and_quantise(bunch):
             for j in range(bunch * BUNCH, (bunch + 1) * BUNCH):
-                grouped = ring.tile([P, HALVES * P * 2 * PAIRS], BF16, align_bytes=64)
-                nc.scalar.copy(
-                    out=grouped[:]
-                    .bitcast(F32)
-                    .rearrange("p (h r u) -> p h r u", h=HALVES, u=PAIRS),
-                    in_=flipped_of[j][:].rearrange("p h u r -> p h r u"),
-                )
-                codes = ring.tile([P, HALVES * P], U32, align_bytes=64)
-                scales = ring.tile([P, HALVES * P], U8, align_bytes=64)
-                nc.vector.quantize_mx(
-                    out=codes[:].bitcast(FP8X4), scales=scales[:], in_=grouped[:]
-                )
-                codes_of[j] = codes
-                scales_of[j] = scales
+                flip(j)
+            for j in range(bunch * BUNCH, (bunch + 1) * BUNCH):
+                group(j, nc.scalar.copy)
+                quantise(j)
 
         def multiply(j):
             partial_of = {}
@@ -247,12 +270,38 @@ def tile_dispatchbyvariable_pa_e_kernel(tc, x, W_words, W_scales, out):
                                 out=out_rows[:, j, cols], in_=partial_of[j][:, cols]
                             )
 
-        with tc.manual_schedule(engines={mybir.EngineType.PE}):
+        head_engines = {
+            mybir.EngineType.PE,
+            mybir.EngineType.Activation,
+            mybir.EngineType.DVE,
+        }
+        with tc.manual_schedule(engines=head_engines):
             keep_warm(WARM_UP)
-            select_and_sort(0)
-            select_and_sort(1)
-            flip_and_quantise(0, fillers=1)
-            flip_and_quantise(1)
+            compare(0)
+            for j in (0, 1):
+                sort_words(j, nc.scalar.copy)
+                make_gates(j)
+            flip(0)
+            flip(1)
+            keep_warm(1)
+            group(0, nc.scalar.copy)
+            compare(1)
+            sort_words(2, nc.vector.tensor_copy)
+            make_gates(2)
+            sort_words(3, nc.scalar.copy)
+            make_gates(3)
+            flip(2)
+            flip(3)
+            keep_warm(1)
+            quantise(0)
+            group(1, nc.scalar.copy)
+            make_picks(0)
+            quantise(1)
+            group(2, nc.scalar.copy)
+            group(3, nc.vector.tensor_copy)
+            make_picks(1)
+            quantise(2)
+            quantise(3)
         for bunch in range(BUNCHES - 1):
             multiply(bunch * BUNCH)
             if bunch + 2 < BUNCHES:

@@ -66,13 +66,16 @@ def tile_dispatchbyvariable_pa_e_kernel(tc, x, W_words, W_scales, out):
                     out=unread[:], lhsT=zeros[:, 0:P], rhs=zeros[:], start=True, stop=True
                 )
 
-        def load_x(bunch):
-            tiles = slice(bunch * BUNCH, (bunch + 1) * BUNCH)
+        def load_tiles(first, beyond):
+            tiles = slice(first, beyond)
             nc.sync.dma_start(out=x_sb[:, tiles, :], in_=x_rows[:, tiles, :])
 
+        def load_x(bunch):
+            load_tiles(bunch * BUNCH, (bunch + 1) * BUNCH)
+
         with tc.manual_schedule(engines={mybir.EngineType.SP}):
-            load_x(0)
-            load_x(1)
+            load_tiles(0, 1)
+            load_tiles(1, 2 * BUNCH)
             for r in range(2):
                 nc.sync.dma_start(
                     out=w_planes[r:P:32, :, :].bitcast(I32),
@@ -101,9 +104,9 @@ def tile_dispatchbyvariable_pa_e_kernel(tc, x, W_words, W_scales, out):
         codes_of = {}
         scales_of = {}
 
-        def compare(bunch):
-            tiles = slice(bunch * BUNCH, (bunch + 1) * BUNCH)
-            shape = [P, BUNCH, len(EDGES)]
+        def compare(first, beyond):
+            tiles = slice(first, beyond)
+            shape = [P, beyond - first, len(EDGES)]
             nc.vector.tensor_tensor(
                 out=above[:, tiles, 1:EXPERTS],
                 in0=x_sb[:, tiles, 0:1].to_broadcast(shape),
@@ -152,7 +155,7 @@ def tile_dispatchbyvariable_pa_e_kernel(tc, x, W_words, W_scales, out):
             )
 
         def select_and_sort(bunch):
-            compare(bunch)
+            compare(bunch * BUNCH, (bunch + 1) * BUNCH)
             for j in range(bunch * BUNCH, (bunch + 1) * BUNCH):
                 sort_words(j, nc.scalar.copy)
                 make_gates(j)
@@ -277,15 +280,16 @@ def tile_dispatchbyvariable_pa_e_kernel(tc, x, W_words, W_scales, out):
         }
         with tc.manual_schedule(engines=head_engines):
             keep_warm(WARM_UP)
-            compare(0)
-            for j in (0, 1):
-                sort_words(j, nc.scalar.copy)
-                make_gates(j)
+            compare(0, 1)
+            sort_words(0, nc.scalar.copy)
+            make_gates(0)
             flip(0)
+            compare(1, 2 * BUNCH)
+            sort_words(1, nc.scalar.copy)
+            make_gates(1)
             flip(1)
             keep_warm(1)
             group(0, nc.scalar.copy)
-            compare(1)
             sort_words(2, nc.vector.tensor_copy)
             make_gates(2)
             sort_words(3, nc.scalar.copy)

@@ -163,8 +163,8 @@ def tile_dispatchbyvariable_pa_e_kernel(tc, x, W_words, W_scales, out):
 
         def flip(j):
             flipped = banks.tile([P, HALVES, PAIRS, P], F32, tag="bank")
-            for half in reversed(range(HALVES)):
-                for u in range(PAIRS):
+            for u in range(PAIRS):
+                for half in reversed(range(HALVES)):
                     nc.tensor.transpose(
                         out=flipped[:, half, u, :],
                         in_=sorted_of[j][:, u, :],
@@ -215,16 +215,16 @@ def tile_dispatchbyvariable_pa_e_kernel(tc, x, W_words, W_scales, out):
                         stop=(half == HALVES - 1),
                     )
                 pick = bank_pick[:, j, bank : bank + 1]
-                if bank < 2:
+                if bank % 2 == 0:
                     partial = partials.tile([P, F], F32)
                     nc.scalar.activation(out=partial[:], in_=sums[:], func=ACT.Copy, scale=pick)
-                    partial_of[bank] = partial
+                    partial_of[bank // 2] = partial
                 else:
                     nc.vector.scalar_tensor_tensor(
-                        out=partial_of[bank - 2][:],
+                        out=partial_of[bank // 2][:],
                         in0=sums[:],
                         scalar=pick,
-                        in1=partial_of[bank - 2][:],
+                        in1=partial_of[bank // 2][:],
                         op0=ALU.mult,
                         op1=ALU.add,
                     )

@@ -284,6 +284,7 @@ def tile_dispatchbyvariable_pa_e_kernel(tc, x, W_words, W_scales, out):
             sort_words(0, nc.scalar.copy)
             make_gates(0)
             flip(0)
+            keep_warm(1)
             compare(1, 2 * BUNCH)
             sort_words(1, nc.scalar.copy)
             make_gates(1)

import concourse.mybir as mybir
from concourse.masks import make_identity

F32 = mybir.dt.float32
BF16 = mybir.dt.bfloat16
I32 = mybir.dt.int32
U32 = mybir.dt.uint32
U8 = mybir.dt.uint8
FP8X4 = mybir.dt.float8_e4m3fn_x4
FP4X4 = mybir.dt.float4_e2m1fn_x4
ALU = mybir.AluOpType
ACT = mybir.ActivationFunctionType

P = 128
TOKENS = 1024
D = 512
F = 512
EDGES = (-1.5, -1.0, -0.5, 0.0, 0.5, 1.0, 1.5)
EXPERTS = len(EDGES) + 1
MIDDLE_EDGE = EDGES[len(EDGES) // 2]
HALVES = 2
BANKS = EXPERTS // HALVES
TILES = TOKENS // P
BUNCH = 2
BUNCHES = TILES // BUNCH
PSUM_BANKS = 8
WARM_UP = 4
PAIRS = 2

FLOPS = 2 * TOKENS * D * F * EXPERTS


def tile_dispatchbyvariable_pa_e_kernel(tc, x, W_words, W_scales, out):
    nc = tc.nc
    x_rows = x.flatten_outer_dims().rearrange("(p j) d -> p j d", j=TILES)
    out_rows = out.flatten_outer_dims().rearrange("(p j) f -> p j f", j=TILES)

    with (
        tc.tile_pool(name="keep", bufs=1) as keep,
        tc.tile_pool(name="ring", bufs=3 * BUNCH) as ring,
        tc.tile_pool(name="partials", bufs=4 * BUNCH) as partials,
        tc.psum_pool(name="banks", bufs=PSUM_BANKS) as banks,
    ):
        x_sb = keep.tile([P, TILES, D], BF16)
        w_words = keep.tile([P, EXPERTS, 2 * F], U8, align_bytes=64)
        w_planes = keep.tile([P, EXPERTS, F], U8, align_bytes=64)
        identity = keep.tile([P, P], F32)
        edges = keep.tile([P, len(EDGES)], F32)
        above = keep.tile([P, TILES, EXPERTS + 1], F32)
        one_hot = keep.tile([P, TILES, EXPERTS], F32)
        bank_pick = keep.tile([P, TILES, BANKS], F32)

        zeros = keep.tile([P, F], BF16)
        nc.gpsimd.memset(zeros[:], 0.0)
        nc.vector.memset(w_planes[:].rearrange("p g n -> p (g n)").bitcast(I32), 0)
        for k, edge in enumerate(EDGES):
            nc.vector.memset(edges[:, k : k + 1], edge)
        nc.vector.memset(above[:, :, 0:1], 1.0)
        nc.vector.memset(above[:, :, EXPERTS : EXPERTS + 1], 0.0)
        make_identity(nc, identity[:])
        unread = banks.tile([P, F], F32, tag="bank")

        def keep_warm(count):
            for i in range(count):
                nc.tensor.matmul(
                    out=unread[:], lhsT=zeros[:, 0:P], rhs=zeros[:], start=True, stop=True
                )

        def load_tiles(first, beyond):
            tiles = slice(first, beyond)
            nc.sync.dma_start(out=x_sb[:, tiles, :], in_=x_rows[:, tiles, :])

        def load_x(bunch):
            load_tiles(bunch * BUNCH, (bunch + 1) * BUNCH)

        with tc.manual_schedule(engines={mybir.EngineType.SP}):
            load_tiles(0, 1)
            load_tiles(1, 2 * BUNCH)
            for r in range(2):
                nc.sync.dma_start(
                    out=w_planes[r:P:32, :, :].bitcast(I32),
                    in_=W_scales[:, r:16:4, :].bitcast(I32).rearrange("g q n -> q g n"),
                )
            for r in range(2, 4):
                for low_q in range(2):
                    nc.sync.dma_start(
                        out=w_planes[32 * low_q + r : P : 64, :, :].bitcast(I32),
                        in_=W_scales[:, 4 * low_q + r : 16 : 8, :]
                        .bitcast(I32)
                        .rearrange("g q n -> q g n"),
                    )
            for bank in range(BANKS):
                nc.sync.dma_start(
                    out=w_words[:, bank:EXPERTS:BANKS, :].bitcast(I32),
                    in_=W_words[bank:EXPERTS:BANKS].bitcast(I32).rearrange("g p b -> p g b"),
                )
            for bunch in range(2, BUNCHES):
                load_x(bunch)

        sorted_of = {}
        gates_of = {}
        flipped_of = {}
        grouped_of = {}
        codes_of = {}
        scales_of = {}

        def compare(first, beyond):
            tiles = slice(first, beyond)
            shape = [P, beyond - first, len(EDGES)]
            nc.vector.tensor_tensor(
                out=above[:, tiles, 1:EXPERTS],
                in0=x_sb[:, tiles, 0:1].to_broadcast(shape),
                in1=edges[:].unsqueeze(1).to_broadcast(shape),
                op=ALU.is_gt,
            )

        def sort_words(j, copy):
            sorted_words = ring.tile([P, PAIRS, P], F32)
            copy(
                out=sorted_words[:],
                in_=x_sb[:, j, :].bitcast(F32).rearrange("p (w u) -> p u w", u=PAIRS),
            )
            sorted_of[j] = sorted_words

        def make_gates(j):
            gates = ring.tile([P, HALVES, P], F32)
            nc.vector.tensor_scalar(
                out=gates[:, 1, :],
                in0=identity[:],
                scalar1=x_sb[:, j, 0:1],
                scalar2=MIDDLE_EDGE,
                op0=ALU.mult,
                op1=ALU.is_gt,
            )
            nc.vector.tensor_scalar(
                out=gates[:, 0, :],
                in0=identity[:],
                scalar1=above[:, j, BANKS : BANKS + 1],
                scalar2=None,
                op0=ALU.is_gt,
            )
            gates_of[j] = gates

        def make_picks(bunch):
            tiles = slice(bunch * BUNCH, (bunch + 1) * BUNCH)
            nc.vector.tensor_sub(
                out=one_hot[:, tiles, :],
                in0=above[:, tiles, 0:EXPERTS],
                in1=above[:, tiles, 1 : EXPERTS + 1],
            )
            nc.vector.tensor_add(
                out=bank_pick[:, tiles, :],
                in0=one_hot[:, tiles, 0:BANKS],
                in1=one_hot[:, tiles, BANKS:EXPERTS],
            )

        def select_and_sort(bunch):
            compare(bunch * BUNCH, (bunch + 1) * BUNCH)
            for j in range(bunch * BUNCH, (bunch + 1) * BUNCH):
                sort_words(j, nc.scalar.copy)
                make_gates(j)
            make_picks(bunch)

        def flip(j):
            flipped = banks.tile([P, HALVES, PAIRS, P], F32, tag="bank")
            for u in range(PAIRS):
                for half in reversed(range(HALVES)):
                    nc.tensor.transpose(
                        out=flipped[:, half, u, :],
                        in_=sorted_of[j][:, u, :],
                        identity=gates_of[j][:, half, :],
                    )
            flipped_of[j] = flipped

        def group(j, copy):
            grouped = ring.tile([P, HALVES * P * 2 * PAIRS], BF16, align_bytes=64)
            copy(
                out=grouped[:]
                .bitcast(F32)
                .rearrange("p (h r u) -> p h r u", h=HALVES, u=PAIRS),
                in_=flipped_of[j][:].rearrange("p h u r -> p h r u"),
            )
            grouped_of[j] = grouped

        def quantise(j):
            codes = ring.tile([P, HALVES * P], U32, align_bytes=64)
            scales = ring.tile([P, HALVES * P], U8, align_bytes=64)
            nc.vector.quantize_mx(
                out=codes[:].bitcast(FP8X4), scales=scales[:], in_=grouped_of[j][:]
            )
            codes_of[j] = codes
            scales_of[j] = scales

        def flip_and_quantise(bunch):
            for j in range(bunch * BUNCH, (bunch + 1) * BUNCH):
                flip(j)
            for j in range(bunch * BUNCH, (bunch + 1) * BUNCH):
                group(j, nc.scalar.copy)
                quantise(j)

        def multiply(j):
            partial_of = {}
            for bank in range(BANKS):
                sums = banks.tile([P, F], F32, tag="bank")
                for half in range(HALVES):
                    tokens = slice(half * P, (half + 1) * P)
                    expert = half * BANKS + bank
                    nc.tensor.matmul_mx(
                        out=sums[:],
                        lhsT=codes_of[j][:, tokens].bitcast(FP8X4),
                        lhsT_scale=scales_of[j][:, tokens],
                        rhs=w_words[:, expert, :].bitcast(FP4X4),
                        rhs_scale=w_planes[:, expert, :],
                        start=(half == 0),
                        stop=(half == HALVES - 1),
                    )
                pick = bank_pick[:, j, bank : bank + 1]
                if bank % 2 == 0:
                    partial = partials.tile([P, F], F32)
                    nc.scalar.activation(out=partial[:], in_=sums[:], func=ACT.Copy, scale=pick)
                    partial_of[bank // 2] = partial
                else:
                    nc.vector.scalar_tensor_tensor(
                        out=partial_of[bank // 2][:],
                        in0=sums[:],
                        scalar=pick,
                        in1=partial_of[bank // 2][:],
                        op0=ALU.mult,
                        op1=ALU.add,
                    )
            nc.gpsimd.tensor_tensor(
                out=partial_of[0][:], in0=partial_of[0][:], in1=partial_of[1][:], op=ALU.add
            )
            nc.sync.dma_start(out=out_rows[:, j, :], in_=partial_of[0][:])

        def multiply_last_bunch(tiles):
            partial_of = {}
            for bank in range(BANKS):
                for j in tiles:
                    sums = banks.tile([P, F], F32, tag="bank")
                    for half in range(HALVES):
                        tokens = slice(half * P, (half + 1) * P)
                        expert = half * BANKS + bank
                        nc.tensor.matmul_mx(
                            out=sums[:],
                            lhsT=codes_of[j][:, tokens].bitcast(FP8X4),
                            lhsT_scale=scales_of[j][:, tokens],
                            rhs=w_words[:, expert, :].bitcast(FP4X4),
                            rhs_scale=w_planes[:, expert, :],
                            start=(half == 0),
                            stop=(half == HALVES - 1),
                        )
                    pick = bank_pick[:, j, bank : bank + 1]
                    if bank == 0:
                        partial = partials.tile([P, F], F32)
                        nc.scalar.activation(
                            out=partial[:], in_=sums[:], func=ACT.Copy, scale=pick
                        )
                        partial_of[j] = partial
                    very_last = bank == BANKS - 1 and j == tiles[-1]
                    pieces = (slice(0, F // 2), slice(F // 2, F)) if very_last else (slice(0, F),)
                    for cols in pieces if bank > 0 else ():
                        nc.vector.scalar_tensor_tensor(
                            out=partial_of[j][:, cols],
                            in0=sums[:, cols],
                            scalar=pick,
                            in1=partial_of[j][:, cols],
                            op0=ALU.mult,
                            op1=ALU.add,
                        )
                        if bank == BANKS - 1:
                            nc.sync.dma_start(
                                out=out_rows[:, j, cols], in_=partial_of[j][:, cols]
                            )

        head_engines = {
            mybir.EngineType.PE,
            mybir.EngineType.Activation,
            mybir.EngineType.DVE,
        }
        with tc.manual_schedule(engines=head_engines):
            keep_warm(WARM_UP)
            compare(0, 1)
            sort_words(0, nc.scalar.copy)
            make_gates(0)
            flip(0)
            keep_warm(1)
            compare(1, 2 * BUNCH)
            sort_words(1, nc.scalar.copy)
            make_gates(1)
            flip(1)
            keep_warm(1)
            group(0, nc.scalar.copy)
            sort_words(2, nc.vector.tensor_copy)
            make_gates(2)
            sort_words(3, nc.scalar.copy)
            make_gates(3)
            flip(2)
            flip(3)
            keep_warm(1)
            quantise(0)
            group(1, nc.scalar.copy)
            make_picks(0)
            quantise(1)
            group(2, nc.scalar.copy)
            group(3, nc.vector.tensor_copy)
            make_picks(1)
            quantise(2)
            quantise(3)
        for bunch in range(BUNCHES - 1):
            multiply(bunch * BUNCH)
            if bunch + 2 < BUNCHES:
                select_and_sort(bunch + 2)
            multiply(bunch * BUNCH + 1)
            if bunch + 2 < BUNCHES:
                flip_and_quantise(bunch + 2)
        multiply_last_bunch((TILES - 2, TILES - 1))
